import numpy as np
import ml_dtypes


def mxq(x, axis, fmt="e4m3"):
    dtype, down = {"e4m3": (ml_dtypes.float8_e4m3fn, 7), "e5m2": (ml_dtypes.float8_e5m2, 14)}[fmt]
    v = np.moveaxis(np.asarray(x, np.float32).astype(ml_dtypes.bfloat16).astype(np.float64), axis, -1)
    blocks = v.reshape(v.shape[:-1] + (-1, 32))
    amax = np.abs(blocks).max(-1, keepdims=True)
    byte = np.maximum(np.where(amax > 0, np.frexp(amax)[1] - 1 + 127, 0) - down, 1)
    scale = np.exp2(byte - 127.0)
    codes = (blocks / scale).astype(np.float32).astype(dtype).astype(np.float64)
    return np.moveaxis((codes * scale).reshape(v.shape), -1, axis)


WIDE = False


def mx_kscale(k):
    if not WIDE:
        return np.ones(k)
    levels = np.array([10, -10, 5, -5, 0])
    a = np.random.permutation(np.resize(levels, k // 512 * 4)).reshape(k // 512, 4)
    idx = np.arange(k)
    return np.exp2(a[idx // 512, idx % 128 // 32])


BF16 = ml_dtypes.bfloat16


def bf(x):
    return np.asarray(x, np.float32).astype(BF16)


def f64(x):
    return np.asarray(x).astype(np.float64)


E2M1 = np.array([0.0, 0.5, 1.0, 1.5, 2.0, 3.0, 4.0, 6.0, -0.0, -0.5, -1.0, -1.5, -2.0, -3.0, -4.0, -6.0])


def pack_weight(w, fmt):
    k, n = w.shape
    w = f64(bf(w)).reshape(k // 32, 32, n)
    amax = np.abs(w).max(1)
    if fmt == "e4m3":
        byte = np.frexp(amax)[1] - 1 + 127 - 7
    else:
        mant, ex = np.frexp(amax / 6.0)
        byte = np.where(mant > 0.5, ex, ex - 1) + 127
    byte = np.clip(np.where(amax > 0, byte, 1), 1, 254)
    scaled = (w * np.exp2(127.0 - byte)[:, None, :]).reshape(k, n).astype(np.float32)
    by_word = np.ascontiguousarray(scaled.reshape(k // 512, 128, 4, n).transpose(0, 1, 3, 2))
    if fmt == "e4m3":
        words = by_word.astype(ml_dtypes.float8_e4m3fn).view(np.uint8)
    else:
        c = by_word.astype(ml_dtypes.float4_e2m1fn).view(np.uint8) & 0xF
        words = c[..., 0::2] | (c[..., 1::2] << 4)
    return np.ascontiguousarray(words), np.ascontiguousarray(byte.astype(np.uint8).reshape(k // 512, 16, n))


def unpack_weight(words, scales, fmt):
    g, p, n, _ = words.shape
    if fmt == "e4m3":
        vals = np.ascontiguousarray(words).view(ml_dtypes.float8_e4m3fn).astype(np.float64)
    else:
        nib = np.empty((g, p, n, 4), np.uint8)
        nib[..., 0::2] = words & 0xF
        nib[..., 1::2] = words >> 4
        vals = E2M1[nib]
    vals = vals * np.repeat(np.exp2(scales.astype(np.float64) - 127.0), 8, axis=1)[..., None]
    return vals.transpose(0, 1, 3, 2).reshape(g * 512, n)


B, L, C, K, D_MODEL, H, D_LLM = 2, 64, 16, 100, 512, 32, 768
D_KEYS = D_MODEL // H
G = H * D_KEYS


def setup_inputs():
    s = mx_kscale(G).reshape(H, D_KEYS)
    attn_ctx = bf(np.random.standard_normal((B, C, L, H, D_KEYS)) * 0.5 * s)
    wo = np.random.standard_normal((C, H, D_KEYS, D_LLM)) * 2.0 / np.sqrt(G) / s[:, :, None]
    wo_words, wo_scales = pack_weight(wo.reshape(C, G, D_LLM).reshape(-1, D_LLM), "e4m3")
    bo = bf(np.random.standard_normal((C, D_LLM)) * 0.5)
    cluster_probs = bf(np.random.uniform(size=(B, L, C)))
    return {
        "attn_ctx": attn_ctx,
        "Wo_words": wo_words,
        "Wo_scales": wo_scales,
        "bo": bo,
        "cluster_probs": cluster_probs,
    }


def reference(attn_ctx, Wo_words, Wo_scales, bo, cluster_probs):
    o = f64(attn_ctx).reshape(B, C, L, G)
    w = unpack_weight(Wo_words, Wo_scales, "e4m3").reshape(C, G, D_LLM)
    proj = mxq(o, 3, "e4m3") @ w
    aligned = proj.transpose(0, 2, 1, 3) + f64(bo)
    return (aligned * f64(cluster_probs)[:, :, :, None]).sum(-2)

@@ -1,0 +1,152 @@
+from contextlib import ExitStack
+
+import concourse.mybir as mybir
+from concourse.masks import make_identity
+
+F32 = mybir.dt.float32
+BF16 = mybir.dt.bfloat16
+I32 = mybir.dt.int32
+U32 = mybir.dt.uint32
+U8 = mybir.dt.uint8
+FP8X4 = mybir.dt.float8_e4m3fn_x4
+MULT = mybir.AluOpType.mult
+ADD = mybir.AluOpType.add
+
+P = 128
+BATCH, CLUSTERS, SEQ, K, D_LLM = 2, 16, 64, 512, 768
+TOKENS = BATCH * SEQ
+PACK = 4
+GROUP = 4
+GROUPS = CLUSTERS // GROUP
+ROWS = 2
+PAIRS = SEQ // ROWS
+QUADRANTS = 4
+WIDE = 512
+PIECES = (("y_wide", 0, WIDE), ("y_narrow", WIDE, D_LLM))
+
+FLOPS = 2 * TOKENS * CLUSTERS * K * D_LLM
+
+
+def tile_model_pa_e_kernel(tc, attn_ctx, Wo_words, Wo_scales, bo, cluster_probs, out):
+    nc = tc.nc
+
+    x_dram = attn_ctx.rearrange("b (g c) (r j) h d -> g (c r) b (j h d)", c=GROUP, j=ROWS)
+    w_dram = Wo_words.rearrange("c p n t -> c p (n t)").bitcast(I32)
+    out_dram = out.rearrange("b l e -> (b l) e")
+
+    with ExitStack() as ctx:
+        const = ctx.enter_context(tc.tile_pool(name="const", bufs=1))
+        per_group = ctx.enter_context(tc.tile_pool(name="per_group", bufs=GROUPS))
+        per_cluster = ctx.enter_context(tc.tile_pool(name="per_cluster", bufs=CLUSTERS))
+        psum_t = ctx.enter_context(tc.psum_pool(name="psum_t", bufs=2))
+        psum_y = ctx.enter_context(tc.psum_pool(name="psum_y", bufs=3))
+
+        x_rows = {}
+        w_planes = {}
+        w_words = {}
+        x_codes = {}
+        x_plane = {}
+
+        def load_x(g):
+            x_rows[g] = per_group.tile([P, BATCH, ROWS * K], BF16, name="x_rows")
+            nc.sync.dma_start(out=x_rows[g][:], in_=x_dram[g])
+
+        def zero_planes(g):
+            w_planes[g] = per_group.tile([P, D_LLM], U8, name="w_planes", align_bytes=64)
+            nc.vector.memset(w_planes[g][:].bitcast(I32), 0)
+
+        def load_planes(g):
+            for q4 in range(QUADRANTS):
+                nc.sync.dma_start(
+                    out=w_planes[g][32 * q4 : 32 * q4 + GROUP * 4, :].bitcast(I32),
+                    in_=Wo_scales[GROUP * g : GROUP * (g + 1), 4 * q4 : 4 * q4 + 4, :].bitcast(I32),
+                )
+
+        def load_words(g):
+            for c in range(GROUP * g, GROUP * (g + 1)):
+                w_words[c] = per_cluster.tile([P, D_LLM], U32, name="w_words", align_bytes=64)
+                nc.sync.dma_start(out=w_words[c][:].bitcast(I32), in_=w_dram[c])
+
+        def quantise_x(g):
+            words = x_rows[g][:].bitcast(F32)
+            half_k = K // 2
+            grouped = per_group.tile([P, GROUP, BATCH, PAIRS, ROWS * PACK], BF16, name="grouped", align_bytes=64)
+            grouped_words = grouped[:].bitcast(F32)
+            for b in range(BATCH):
+                flipped = psum_t.tile([P, ROWS * 2, P], F32, name="flipped")
+                for j in range(ROWS):
+                    for u in range(2):
+                        nc.tensor.transpose(
+                            flipped[:, 2 * j + u, :],
+                            words[:, b, half_k * j + u : half_k * (j + 1) : 2],
+                            identity[:],
+                        )
+                nc.scalar.copy(out=grouped_words[:, :, b, :, :], in_=flipped[:].rearrange("p a (c r) -> p c r a", c=GROUP))
+            x_codes[g] = per_group.tile([P, GROUP * TOKENS], U32, name="x_codes", align_bytes=64)
+            x_plane[g] = per_group.tile([P, GROUP * TOKENS], U8, name="x_plane", align_bytes=64)
+            nc.vector.quantize_mx(
+                out=x_codes[g][:].bitcast(FP8X4),
+                scales=x_plane[g][:],
+                in_=grouped[:].rearrange("p c b r v -> p (c b r v)"),
+            )
+
+        def project(g, i):
+            c = GROUP * g + i
+            tokens = slice(TOKENS * i, TOKENS * (i + 1))
+            for name, lo, hi in PIECES:
+                cols = slice(lo, hi)
+                y = psum_y.tile([P, hi - lo], F32, name=name)
+                nc.tensor.matmul_mx(
+                    out=y[:],
+                    lhsT=x_codes[g][:, tokens].bitcast(FP8X4),
+                    lhsT_scale=x_plane[g][:, tokens],
+                    rhs=w_words[c][:, cols].bitcast(FP8X4),
+                    rhs_scale=w_planes[g][4 * i : P, cols],
+                    start=True,
+                    stop=True,
+                )
+                nc.vector.scalar_tensor_tensor(
+                    out=fused[:, cols], in0=y[:], scalar=probs[:, c : c + 1], in1=fused[:, cols], op0=MULT, op1=ADD
+                )
+
+        for g in range(GROUPS):
+            zero_planes(g)
+        load_x(0)
+        load_planes(0)
+        for g in range(GROUPS):
+            if g + 1 < GROUPS:
+                load_x(g + 1)
+            load_words(g)
+            if g + 1 < GROUPS:
+                load_planes(g + 1)
+
+        identity = const.tile([P, P], F32, name="identity")
+        make_identity(nc, identity[:])
+        probs_bf = const.tile([TOKENS, CLUSTERS], BF16, name="probs_bf")
+        nc.scalar.dma_start(out=probs_bf[:], in_=cluster_probs.rearrange("b l c -> (b l) c"))
+        bo_rows = const.tile([P, D_LLM], BF16, name="bo_rows")
+        nc.vector.memset(bo_rows[:], 0.0)
+        nc.scalar.dma_start(out=bo_rows[0:CLUSTERS, :], in_=bo)
+        probs = const.tile([TOKENS, P], F32, name="probs")
+        nc.vector.memset(probs[:], 0.0)
+        nc.vector.tensor_copy(out=probs[:, 0:CLUSTERS], in_=probs_bf[:])
+
+        probs_flipped = psum_t.tile([P, ROWS * 2, P], F32, name="flipped")
+        nc.tensor.transpose(probs_flipped[:, 0, :], probs[:], identity[:])
+        probs_t = const.tile([P, TOKENS], BF16, name="probs_t")
+        nc.vector.tensor_copy(out=probs_t[:], in_=probs_flipped[:, 0, :])
+        fused = const.tile([TOKENS, D_LLM], F32, name="fused")
+        for name, lo, hi in PIECES:
+            bias = psum_y.tile([P, hi - lo], F32, name=name)
+            nc.tensor.matmul(out=bias[:], lhsT=probs_t[:], rhs=bo_rows[:, lo:hi], start=True, stop=True)
+            nc.scalar.copy(out=fused[:, lo:hi], in_=bias[:])
+
+        quantise_x(0)
+        for g in range(GROUPS):
+            if g + 1 < GROUPS:
+                quantise_x(g + 1)
+            for i in range(GROUP):
+                project(g, i)
+
+        for name, lo, hi in PIECES:
+            nc.sync.dma_start(out=out_dram[:, lo:hi], in_=fused[:, lo:hi])

@@ -11,6 +11,7 @@ U8 = mybir.dt.uint8
 FP8X4 = mybir.dt.float8_e4m3fn_x4
 MULT = mybir.AluOpType.mult
 ADD = mybir.AluOpType.add
+COPY = mybir.ActivationFunctionType.Copy
 
 P = 128
 BATCH, CLUSTERS, SEQ, K, D_LLM = 2, 16, 64, 512, 768
@@ -40,6 +41,7 @@ def tile_model_pa_e_kernel(tc, attn_ctx, Wo_words, Wo_scales, bo, cluster_probs,
         per_cluster = ctx.enter_context(tc.tile_pool(name="per_cluster", bufs=CLUSTERS))
         psum_t = ctx.enter_context(tc.psum_pool(name="psum_t", bufs=2))
         psum_y = ctx.enter_context(tc.psum_pool(name="psum_y", bufs=3))
+        weighted_pool = ctx.enter_context(tc.tile_pool(name="weighted_pool", bufs=3))
 
         x_rows = {}
         w_planes = {}
@@ -105,9 +107,14 @@ def tile_model_pa_e_kernel(tc, attn_ctx, Wo_words, Wo_scales, bo, cluster_probs,
                     start=True,
                     stop=True,
                 )
-                nc.vector.scalar_tensor_tensor(
-                    out=fused[:, cols], in0=y[:], scalar=probs[:, c : c + 1], in1=fused[:, cols], op0=MULT, op1=ADD
-                )
+                if name == "y_wide":
+                    nc.vector.scalar_tensor_tensor(
+                        out=fused[name][:], in0=y[:], scalar=probs[:, c : c + 1], in1=fused[name][:], op0=MULT, op1=ADD
+                    )
+                else:
+                    weighted = weighted_pool.tile([P, hi - lo], F32, name="weighted")
+                    nc.scalar.activation(out=weighted[:], in_=y[:], func=COPY, scale=probs[:, c : c + 1])
+                    nc.gpsimd.tensor_tensor(out=fused[name][:], in0=fused[name][:], in1=weighted[:], op=ADD)
 
         for g in range(GROUPS):
             zero_planes(g)
@@ -135,11 +142,12 @@ def tile_model_pa_e_kernel(tc, attn_ctx, Wo_words, Wo_scales, bo, cluster_probs,
         nc.tensor.transpose(probs_flipped[:, 0, :], probs[:], identity[:])
         probs_t = const.tile([P, TOKENS], BF16, name="probs_t")
         nc.vector.tensor_copy(out=probs_t[:], in_=probs_flipped[:, 0, :])
-        fused = const.tile([TOKENS, D_LLM], F32, name="fused")
+        fused = {}
         for name, lo, hi in PIECES:
             bias = psum_y.tile([P, hi - lo], F32, name=name)
             nc.tensor.matmul(out=bias[:], lhsT=probs_t[:], rhs=bo_rows[:, lo:hi], start=True, stop=True)
-            nc.scalar.copy(out=fused[:, lo:hi], in_=bias[:])
+            fused[name] = const.tile([TOKENS, hi - lo], F32, name="fused_" + name)
+            nc.scalar.copy(out=fused[name][:], in_=bias[:])
 
         quantise_x(0)
         for g in range(GROUPS):
@@ -149,4 +157,4 @@ def tile_model_pa_e_kernel(tc, attn_ctx, Wo_words, Wo_scales, bo, cluster_probs,
                 project(g, i)
 
         for name, lo, hi in PIECES:
-            nc.sync.dma_start(out=out_dram[:, lo:hi], in_=fused[:, lo:hi])
+            nc.sync.dma_start(out=out_dram[:, lo:hi], in_=fused[name][:])

@@ -23,6 +23,7 @@ ROWS = 2
 PAIRS = SEQ // ROWS
 QUADRANTS = 4
 WIDE = 512
+HALF = WIDE // 2
 PIECES = (("y_wide", 0, WIDE), ("y_narrow", WIDE, D_LLM))
 
 FLOPS = 2 * TOKENS * CLUSTERS * K * D_LLM
@@ -46,6 +47,7 @@ def tile_model_pa_e_kernel(tc, attn_ctx, Wo_words, Wo_scales, bo, cluster_probs,
         x_rows = {}
         w_planes = {}
         w_words = {}
+        x_grouped = {}
         x_codes = {}
         x_plane = {}
 
@@ -69,10 +71,11 @@ def tile_model_pa_e_kernel(tc, attn_ctx, Wo_words, Wo_scales, bo, cluster_probs,
                 w_words[c] = per_cluster.tile([P, D_LLM], U32, name="w_words", align_bytes=64)
                 nc.sync.dma_start(out=w_words[c][:].bitcast(I32), in_=w_dram[c])
 
-        def quantise_x(g):
+        def flip_x(g):
             words = x_rows[g][:].bitcast(F32)
             half_k = K // 2
             grouped = per_group.tile([P, GROUP, BATCH, PAIRS, ROWS * PACK], BF16, name="grouped", align_bytes=64)
+            x_grouped[g] = grouped
             grouped_words = grouped[:].bitcast(F32)
             for b in range(BATCH):
                 flipped = psum_t.tile([P, ROWS * 2, P], F32, name="flipped")
@@ -84,12 +87,14 @@ def tile_model_pa_e_kernel(tc, attn_ctx, Wo_words, Wo_scales, bo, cluster_probs,
                             identity[:],
                         )
                 nc.scalar.copy(out=grouped_words[:, :, b, :, :], in_=flipped[:].rearrange("p a (c r) -> p c r a", c=GROUP))
+
+        def quantise_x(g):
             x_codes[g] = per_group.tile([P, GROUP * TOKENS], U32, name="x_codes", align_bytes=64)
             x_plane[g] = per_group.tile([P, GROUP * TOKENS], U8, name="x_plane", align_bytes=64)
             nc.vector.quantize_mx(
                 out=x_codes[g][:].bitcast(FP8X4),
                 scales=x_plane[g][:],
-                in_=grouped[:].rearrange("p c b r v -> p (c b r v)"),
+                in_=x_grouped[g][:].rearrange("p c b r v -> p (c b r v)"),
             )
 
         def project(g, i):
@@ -108,6 +113,16 @@ def tile_model_pa_e_kernel(tc, attn_ctx, Wo_words, Wo_scales, bo, cluster_probs,
                     stop=True,
                 )
                 if name == "y_wide":
+                    for half in (slice(0, HALF), slice(HALF, WIDE)):
+                        nc.vector.scalar_tensor_tensor(
+                            out=fused[name][:, half],
+                            in0=y[:, half],
+                            scalar=probs[:, c : c + 1],
+                            in1=fused[name][:, half],
+                            op0=MULT,
+                            op1=ADD,
+                        )
+                elif i == GROUP - 1:
                     nc.vector.scalar_tensor_tensor(
                         out=fused[name][:], in0=y[:], scalar=probs[:, c : c + 1], in1=fused[name][:], op0=MULT, op1=ADD
                     )
@@ -149,12 +164,16 @@ def tile_model_pa_e_kernel(tc, attn_ctx, Wo_words, Wo_scales, bo, cluster_probs,
             fused[name] = const.tile([TOKENS, hi - lo], F32, name="fused_" + name)
             nc.scalar.copy(out=fused[name][:], in_=bias[:])
 
-        quantise_x(0)
-        for g in range(GROUPS):
-            if g + 1 < GROUPS:
-                quantise_x(g + 1)
-            for i in range(GROUP):
-                project(g, i)
+        with tc.manual_schedule():
+            flip_x(0)
+            quantise_x(0)
+            for g in range(GROUPS):
+                if g + 1 < GROUPS:
+                    flip_x(g + 1)
+                for i in range(GROUP):
+                    if i == GROUP // 2 and g + 1 < GROUPS:
+                        quantise_x(g + 1)
+                    project(g, i)
 
         for name, lo, hi in PIECES:
             nc.sync.dma_start(out=out_dram[:, lo:hi], in_=fused[name][:])

@@ -135,9 +135,10 @@ def tile_model_pa_e_kernel(tc, attn_ctx, Wo_words, Wo_scales, bo, cluster_probs,
             zero_planes(g)
         load_x(0)
         load_planes(0)
+        load_x(1)
         for g in range(GROUPS):
-            if g + 1 < GROUPS:
-                load_x(g + 1)
+            if g + 2 < GROUPS:
+                load_x(g + 2)
             load_words(g)
             if g + 1 < GROUPS:
                 load_planes(g + 1)
@@ -165,15 +166,16 @@ def tile_model_pa_e_kernel(tc, attn_ctx, Wo_words, Wo_scales, bo, cluster_probs,
             nc.scalar.copy(out=fused[name][:], in_=bias[:])
 
         with tc.manual_schedule():
-            flip_x(0)
-            quantise_x(0)
+            for g in range(2):
+                flip_x(g)
+                quantise_x(g)
             for g in range(GROUPS):
-                if g + 1 < GROUPS:
-                    flip_x(g + 1)
+                if g + 2 < GROUPS:
+                    flip_x(g + 2)
                 for i in range(GROUP):
-                    if i == GROUP // 2 and g + 1 < GROUPS:
-                        quantise_x(g + 1)
                     project(g, i)
+                if g + 2 < GROUPS:
+                    quantise_x(g + 2)
 
         for name, lo, hi in PIECES:
             nc.sync.dma_start(out=out_dram[:, lo:hi], in_=fused[name][:])

@@ -26,6 +26,8 @@ WIDE = 512
 HALF = WIDE // 2
 PIECES = (("y_wide", 0, WIDE), ("y_narrow", WIDE, D_LLM))
 
+LOAD_CLUSTERS = (2, 2, 2, 1)
+
 FLOPS = 2 * TOKENS * CLUSTERS * K * D_LLM
 
 
@@ -33,13 +35,12 @@ def tile_model_pa_e_kernel(tc, attn_ctx, Wo_words, Wo_scales, bo, cluster_probs,
     nc = tc.nc
 
     x_dram = attn_ctx.rearrange("b (g c) (r j) h d -> g (c r) b (j h d)", c=GROUP, j=ROWS)
-    w_dram = Wo_words.rearrange("c p n t -> c p (n t)").bitcast(I32)
+    w_dram = Wo_words.rearrange("c p n t -> p c (n t)").bitcast(I32)
     out_dram = out.rearrange("b l e -> (b l) e")
 
     with ExitStack() as ctx:
         const = ctx.enter_context(tc.tile_pool(name="const", bufs=1))
         per_group = ctx.enter_context(tc.tile_pool(name="per_group", bufs=GROUPS))
-        per_cluster = ctx.enter_context(tc.tile_pool(name="per_cluster", bufs=CLUSTERS))
         psum_t = ctx.enter_context(tc.psum_pool(name="psum_t", bufs=2))
         psum_y = ctx.enter_context(tc.psum_pool(name="psum_y", bufs=3))
         weighted_pool = ctx.enter_context(tc.tile_pool(name="weighted_pool", bufs=3))
@@ -67,9 +68,12 @@ def tile_model_pa_e_kernel(tc, attn_ctx, Wo_words, Wo_scales, bo, cluster_probs,
                 )
 
         def load_words(g):
-            for c in range(GROUP * g, GROUP * (g + 1)):
-                w_words[c] = per_cluster.tile([P, D_LLM], U32, name="w_words", align_bytes=64)
-                nc.sync.dma_start(out=w_words[c][:].bitcast(I32), in_=w_dram[c])
+            step = LOAD_CLUSTERS[g]
+            for c in range(GROUP * g, GROUP * (g + 1), step):
+                words = const.tile([P, step, D_LLM], U32, name="w_words_" + str(c), align_bytes=64)
+                nc.sync.dma_start(out=words[:].bitcast(I32), in_=w_dram[:, c : c + step, :])
+                for j in range(step):
+                    w_words[c + j] = words[:, j, :]
 
         def flip_x(g):
             words = x_rows[g][:].bitcast(F32)

@@ -67,11 +67,15 @@ def tile_model_pa_e_kernel(tc, attn_ctx, Wo_words, Wo_scales, bo, cluster_probs,
                     in_=Wo_scales[GROUP * g : GROUP * (g + 1), 4 * q4 : 4 * q4 + 4, :].bitcast(I32),
                 )
 
-        def load_words(g):
+        def load_words(g, first, end):
             step = LOAD_CLUSTERS[g]
-            for c in range(GROUP * g, GROUP * (g + 1), step):
+            for c in range(GROUP * g + first, GROUP * g + end, step):
                 words = const.tile([P, step, D_LLM], U32, name="w_words_" + str(c), align_bytes=64)
-                nc.sync.dma_start(out=words[:].bitcast(I32), in_=w_dram[:, c : c + step, :])
+                if c == CLUSTERS - 1:
+                    for name, lo, hi in PIECES:
+                        nc.sync.dma_start(out=words[:, :, lo:hi].bitcast(I32), in_=w_dram[:, c : c + step, lo:hi])
+                else:
+                    nc.sync.dma_start(out=words[:].bitcast(I32), in_=w_dram[:, c : c + step, :])
                 for j in range(step):
                     w_words[c + j] = words[:, j, :]
 
@@ -141,9 +145,10 @@ def tile_model_pa_e_kernel(tc, attn_ctx, Wo_words, Wo_scales, bo, cluster_probs,
         load_planes(0)
         load_x(1)
         for g in range(GROUPS):
+            load_words(g, 0, GROUP // 2)
             if g + 2 < GROUPS:
                 load_x(g + 2)
-            load_words(g)
+            load_words(g, GROUP // 2, GROUP)
             if g + 1 < GROUPS:
                 load_planes(g + 1)
 
@@ -174,12 +179,12 @@ def tile_model_pa_e_kernel(tc, attn_ctx, Wo_words, Wo_scales, bo, cluster_probs,
                 flip_x(g)
                 quantise_x(g)
             for g in range(GROUPS):
-                if g + 2 < GROUPS:
-                    flip_x(g + 2)
                 for i in range(GROUP):
+                    if i == GROUP // 2 and g + 2 < GROUPS:
+                        flip_x(g + 2)
                     project(g, i)
                 if g + 2 < GROUPS:
                     quantise_x(g + 2)
 
-        for name, lo, hi in PIECES:
-            nc.sync.dma_start(out=out_dram[:, lo:hi], in_=fused[name][:])
+        for queue, (name, lo, hi) in zip((nc.sync, nc.scalar), PIECES):
+            queue.dma_start(out=out_dram[:, lo:hi], in_=fused[name][:])

from contextlib import ExitStack

import concourse.mybir as mybir
from concourse.masks import make_identity

F32 = mybir.dt.float32
BF16 = mybir.dt.bfloat16
I32 = mybir.dt.int32
U32 = mybir.dt.uint32
U8 = mybir.dt.uint8
FP8X4 = mybir.dt.float8_e4m3fn_x4
MULT = mybir.AluOpType.mult
ADD = mybir.AluOpType.add
COPY = mybir.ActivationFunctionType.Copy

P = 128
BATCH, CLUSTERS, SEQ, K, D_LLM = 2, 16, 64, 512, 768
TOKENS = BATCH * SEQ
PACK = 4
GROUP = 4
GROUPS = CLUSTERS // GROUP
ROWS = 2
PAIRS = SEQ // ROWS
QUADRANTS = 4
WIDE = 512
HALF = WIDE // 2
PIECES = (("y_wide", 0, WIDE), ("y_narrow", WIDE, D_LLM))

LOAD_CLUSTERS = (2, 2, 2, 1)

FLOPS = 2 * TOKENS * CLUSTERS * K * D_LLM


def tile_model_pa_e_kernel(tc, attn_ctx, Wo_words, Wo_scales, bo, cluster_probs, out):
    nc = tc.nc

    x_dram = attn_ctx.rearrange("b (g c) (r j) h d -> g (c r) b (j h d)", c=GROUP, j=ROWS)
    w_dram = Wo_words.rearrange("c p n t -> p c (n t)").bitcast(I32)
    out_dram = out.rearrange("b l e -> (b l) e")

    with ExitStack() as ctx:
        const = ctx.enter_context(tc.tile_pool(name="const", bufs=1))
        per_group = ctx.enter_context(tc.tile_pool(name="per_group", bufs=GROUPS))
        psum_t = ctx.enter_context(tc.psum_pool(name="psum_t", bufs=2))
        psum_y = ctx.enter_context(tc.psum_pool(name="psum_y", bufs=3))
        weighted_pool = ctx.enter_context(tc.tile_pool(name="weighted_pool", bufs=3))

        x_rows = {}
        w_planes = {}
        w_words = {}
        x_grouped = {}
        x_codes = {}
        x_plane = {}

        def load_x(g):
            x_rows[g] = per_group.tile([P, BATCH, ROWS * K], BF16, name="x_rows")
            nc.sync.dma_start(out=x_rows[g][:], in_=x_dram[g])

        def zero_planes(g):
            w_planes[g] = per_group.tile([P, D_LLM], U8, name="w_planes", align_bytes=64)
            nc.vector.memset(w_planes[g][:].bitcast(I32), 0)

        def load_planes(g):
            for q4 in range(QUADRANTS):
                nc.sync.dma_start(
                    out=w_planes[g][32 * q4 : 32 * q4 + GROUP * 4, :].bitcast(I32),
                    in_=Wo_scales[GROUP * g : GROUP * (g + 1), 4 * q4 : 4 * q4 + 4, :].bitcast(I32),
                )

        def load_words(g, first, end):
            step = LOAD_CLUSTERS[g]
            for c in range(GROUP * g + first, GROUP * g + end, step):
                words = const.tile([P, step, D_LLM], U32, name="w_words_" + str(c), align_bytes=64)
                if c == CLUSTERS - 1:
                    for name, lo, hi in PIECES:
                        nc.sync.dma_start(out=words[:, :, lo:hi].bitcast(I32), in_=w_dram[:, c : c + step, lo:hi])
                else:
                    nc.sync.dma_start(out=words[:].bitcast(I32), in_=w_dram[:, c : c + step, :])
                for j in range(step):
                    w_words[c + j] = words[:, j, :]

        def flip_x(g):
            words = x_rows[g][:].bitcast(F32)
            half_k = K // 2
            grouped = per_group.tile([P, GROUP, BATCH, PAIRS, ROWS * PACK], BF16, name="grouped", align_bytes=64)
            x_grouped[g] = grouped
            grouped_words = grouped[:].bitcast(F32)
            for b in range(BATCH):
                flipped = psum_t.tile([P, ROWS * 2, P], F32, name="flipped")
                for j in range(ROWS):
                    for u in range(2):
                        nc.tensor.transpose(
                            flipped[:, 2 * j + u, :],
                            words[:, b, half_k * j + u : half_k * (j + 1) : 2],
                            identity[:],
                        )
                nc.scalar.copy(out=grouped_words[:, :, b, :, :], in_=flipped[:].rearrange("p a (c r) -> p c r a", c=GROUP))

        def quantise_x(g):
            x_codes[g] = per_group.tile([P, GROUP * TOKENS], U32, name="x_codes", align_bytes=64)
            x_plane[g] = per_group.tile([P, GROUP * TOKENS], U8, name="x_plane", align_bytes=64)
            nc.vector.quantize_mx(
                out=x_codes[g][:].bitcast(FP8X4),
                scales=x_plane[g][:],
                in_=x_grouped[g][:].rearrange("p c b r v -> p (c b r v)"),
            )

        def project(g, i):
            c = GROUP * g + i
            tokens = slice(TOKENS * i, TOKENS * (i + 1))
            for name, lo, hi in PIECES:
                cols = slice(lo, hi)
                y = psum_y.tile([P, hi - lo], F32, name=name)
                nc.tensor.matmul_mx(
                    out=y[:],
                    lhsT=x_codes[g][:, tokens].bitcast(FP8X4),
                    lhsT_scale=x_plane[g][:, tokens],
                    rhs=w_words[c][:, cols].bitcast(FP8X4),
                    rhs_scale=w_planes[g][4 * i : P, cols],
                    start=True,
                    stop=True,
                )
                if name == "y_wide":
                    for half in (slice(0, HALF), slice(HALF, WIDE)):
                        nc.vector.scalar_tensor_tensor(
                            out=fused[name][:, half],
                            in0=y[:, half],
                            scalar=probs[:, c : c + 1],
                            in1=fused[name][:, half],
                            op0=MULT,
                            op1=ADD,
                        )
                elif i == GROUP - 1:
                    nc.vector.scalar_tensor_tensor(
                        out=fused[name][:], in0=y[:], scalar=probs[:, c : c + 1], in1=fused[name][:], op0=MULT, op1=ADD
                    )
                else:
                    weighted = weighted_pool.tile([P, hi - lo], F32, name="weighted")
                    nc.scalar.activation(out=weighted[:], in_=y[:], func=COPY, scale=probs[:, c : c + 1])
                    nc.gpsimd.tensor_tensor(out=fused[name][:], in0=fused[name][:], in1=weighted[:], op=ADD)

        for g in range(GROUPS):
            zero_planes(g)
        load_x(0)
        load_planes(0)
        load_x(1)
        for g in range(GROUPS):
            load_words(g, 0, GROUP // 2)
            if g + 2 < GROUPS:
                load_x(g + 2)
            load_words(g, GROUP // 2, GROUP)
            if g + 1 < GROUPS:
                load_planes(g + 1)

        identity = const.tile([P, P], F32, name="identity")
        make_identity(nc, identity[:])
        probs_bf = const.tile([TOKENS, CLUSTERS], BF16, name="probs_bf")
        nc.scalar.dma_start(out=probs_bf[:], in_=cluster_probs.rearrange("b l c -> (b l) c"))
        bo_rows = const.tile([P, D_LLM], BF16, name="bo_rows")
        nc.vector.memset(bo_rows[:], 0.0)
        nc.scalar.dma_start(out=bo_rows[0:CLUSTERS, :], in_=bo)
        probs = const.tile([TOKENS, P], F32, name="probs")
        nc.vector.memset(probs[:], 0.0)
        nc.vector.tensor_copy(out=probs[:, 0:CLUSTERS], in_=probs_bf[:])

        probs_flipped = psum_t.tile([P, ROWS * 2, P], F32, name="flipped")
        nc.tensor.transpose(probs_flipped[:, 0, :], probs[:], identity[:])
        probs_t = const.tile([P, TOKENS], BF16, name="probs_t")
        nc.vector.tensor_copy(out=probs_t[:], in_=probs_flipped[:, 0, :])
        fused = {}
        for name, lo, hi in PIECES:
            bias = psum_y.tile([P, hi - lo], F32, name=name)
            nc.tensor.matmul(out=bias[:], lhsT=probs_t[:], rhs=bo_rows[:, lo:hi], start=True, stop=True)
            fused[name] = const.tile([TOKENS, hi - lo], F32, name="fused_" + name)
            nc.scalar.copy(out=fused[name][:], in_=bias[:])

        with tc.manual_schedule():
            for g in range(2):
                flip_x(g)
                quantise_x(g)
            for g in range(GROUPS):
                for i in range(GROUP):
                    if i == GROUP // 2 and g + 2 < GROUPS:
                        flip_x(g + 2)
                    project(g, i)
                if g + 2 < GROUPS:
                    quantise_x(g + 2)

        for queue, (name, lo, hi) in zip((nc.sync, nc.scalar), PIECES):
            queue.dma_start(out=out_dram[:, lo:hi], in_=fused[name][:])
